import numpy as np
import ml_dtypes


def mxq(x, axis, fmt="e4m3"):
    dtype, down = {"e4m3": (ml_dtypes.float8_e4m3fn, 7), "e5m2": (ml_dtypes.float8_e5m2, 14)}[fmt]
    v = np.moveaxis(np.asarray(x, np.float32).astype(ml_dtypes.bfloat16).astype(np.float64), axis, -1)
    blocks = v.reshape(v.shape[:-1] + (-1, 32))
    amax = np.abs(blocks).max(-1, keepdims=True)
    byte = np.maximum(np.where(amax > 0, np.frexp(amax)[1] - 1 + 127, 0) - down, 1)
    scale = np.exp2(byte - 127.0)
    codes = (blocks / scale).astype(np.float32).astype(dtype).astype(np.float64)
    return np.moveaxis((codes * scale).reshape(v.shape), -1, axis)


WIDE = False


def mx_kscale(k):
    if not WIDE:
        return np.ones(k)
    levels = np.array([10, -10, 5, -5, 0])
    a = np.random.permutation(np.resize(levels, k // 512 * 4)).reshape(k // 512, 4)
    idx = np.arange(k)
    return np.exp2(a[idx // 512, idx % 128 // 32])


BF16 = ml_dtypes.bfloat16


def bf(x):
    return np.asarray(x, np.float32).astype(BF16)


def f64(x):
    return np.asarray(x).astype(np.float64)


B, DI, DH = 4096, 1024, 128


def sigmoid(v):
    return 1.0 / (1.0 + np.exp(-v))


def setup_inputs():
    s = mx_kscale(DI)
    n = np.random.standard_normal
    a, c = 0.7 / np.sqrt(DI), 0.7 / np.sqrt(DH)
    keep = np.random.uniform(size=B) < 0.9
    return {
        "x": bf(n((B, DI)) * s),
        "h_minors": bf(n((B, DH))),
        "c_minors": bf(n((B, DH))),
        "s0": bf(n((B, DH))),
        "s1": bf(n((B, DH))),
        "s2": bf(n((B, DH))),
        "mask": bf(keep * (0.5 + 0.5 * np.random.uniform(size=B))),
        "weight_ih": bf(n((7 * DH, DI)) * a / s),
        "bias_ih": bf(n(7 * DH) * 0.3),
        "weight_hh": bf(n((4 * DH, DH)) * c),
        "bias_hh": bf(n(4 * DH) * 0.3),
        "weight_sh0": bf(n((DH, DH)) * c),
        "bias_sh0": bf(n(DH) * 0.3),
        "weight_sh1": bf(n((DH, DH)) * c),
        "bias_sh1": bf(n(DH) * 0.3),
        "weight_sh2": bf(n((DH, DH)) * c),
        "bias_sh2": bf(n(DH) * 0.3),
    }


def reference(x, h_minors, c_minors, s0, s1, s2, mask, weight_ih, bias_ih, weight_hh, bias_hh,
              weight_sh0, bias_sh0, weight_sh1, bias_sh1, weight_sh2, bias_sh2):
    d = DH
    m = f64(mask)[:, None]

    tmp = (mxq(f64(x), 1, "e4m3") @ mxq(f64(weight_ih), 1, "e4m3").T) + f64(bias_ih)
    tmp2 = f64(h_minors) @ f64(weight_hh).T + f64(bias_hh)
    tmp3 = np.concatenate([
        f64(s0) @ f64(weight_sh0).T + f64(bias_sh0),
        f64(s1) @ f64(weight_sh1).T + f64(bias_sh1),
        f64(s2) @ f64(weight_sh2).T + f64(bias_sh2),
    ], axis=1)

    tmp_in, tmp_s = tmp[:, :4 * d], tmp[:, 4 * d:]
    pre = tmp_in + tmp2
    ifo = sigmoid(pre[:, :3 * d])
    c_hat = pre[:, 3 * d:]
    i_g, f_g, o_g = ifo[:, :d], ifo[:, d:2 * d], ifo[:, 2 * d:]

    c_t = (f_g * f64(c_minors) + i_g * np.tanh(c_hat)) * m
    tc = np.tanh(c_t) * m
    h = o_g * tc

    bg = sigmoid(tmp_s + tmp3)
    b0, b1, b2 = bg[:, :d], bg[:, d:2 * d], bg[:, 2 * d:]

    s_0 = (b0 + 1.0 - o_g) * tc
    s_1 = (b1 + 2.0 - o_g - s_0) * 0.5 * tc
    s_2 = (b2 + 3.0 - o_g - (2.0 * s_0 + s_1)) * (1.0 / 3.0) * tc

    return (h, c_t, s_0, s_1, s_2)

@@ -1,0 +1,297 @@
+from contextlib import ExitStack
+
+import concourse.mybir as mybir
+from concourse.masks import make_identity
+
+F32 = mybir.dt.float32
+BF16 = mybir.dt.bfloat16
+U32 = mybir.dt.uint32
+U8 = mybir.dt.uint8
+FP8X4 = mybir.dt.float8_e4m3fn_x4
+ACT = mybir.ActivationFunctionType
+ALU = mybir.AluOpType
+
+P = 128
+B = 4096
+DI = 1024
+DH = 128
+N_GATES = 7
+I_G = 0
+F_G = 1
+O_G = 2
+C_HAT = 3
+B0_G = 4
+ROWS_PER_PARTITION = B // P
+TILES = 4
+BLOCK = TILES * P
+N_BLOCKS = B // BLOCK
+PACK = 4
+PASSES = DI // (P * PACK)
+HALVES = 2
+CHUNK = PASSES * P
+N_SMALL = 5
+C_SLOT = 4
+
+FLOPS = 2 * B * N_GATES * DH * (DI + DH)
+
+
+def tile_share_lstm_cell_pa_t_kernel(
+    tc, x, h_minors, c_minors, s0, s1, s2, mask,
+    weight_ih, bias_ih, weight_hh, bias_hh,
+    weight_sh0, bias_sh0, weight_sh1, bias_sh1, weight_sh2, bias_sh2,
+    out_0, out_1, out_2, out_3, out_4,
+):
+    nc = tc.nc
+
+    x_rows = x.rearrange("(p j) k -> p j k", j=ROWS_PER_PARTITION)
+    small_rows = [
+        a.rearrange("(p j) d -> p j d", j=ROWS_PER_PARTITION)
+        for a in (h_minors, s0, s1, s2, c_minors)
+    ]
+    out_rows = [
+        a.rearrange("(p j) d -> p j d", j=ROWS_PER_PARTITION)
+        for a in (out_0, out_1, out_2, out_3, out_4)
+    ]
+
+    with ExitStack() as stack:
+        const = stack.enter_context(tc.tile_pool(name="const", bufs=1))
+        x_pool = stack.enter_context(tc.tile_pool(name="x_pool", bufs=3))
+        small_pool = stack.enter_context(tc.tile_pool(name="small_pool", bufs=4))
+        operand_pool = stack.enter_context(tc.tile_pool(name="operand_pool", bufs=2))
+        pre_pool = stack.enter_context(tc.tile_pool(name="pre_pool", bufs=4))
+        gate_pool = stack.enter_context(tc.tile_pool(name="gate_pool", bufs=2))
+        finish_pool = stack.enter_context(tc.tile_pool(name="finish_pool", bufs=2))
+        out_pool = stack.enter_context(tc.tile_pool(name="out_pool", bufs=2))
+        psum_in = stack.enter_context(tc.psum_pool(name="psum_in", bufs=2))
+        psum_plain = stack.enter_context(tc.psum_pool(name="psum_plain", bufs=2))
+        psum_mx = stack.enter_context(tc.psum_pool(name="psum_mx", bufs=2))
+        psum_back = stack.enter_context(tc.psum_pool(name="psum_back", bufs=2))
+
+        ident_f32 = const.tile([P, P], F32, name="ident_f32")
+        make_identity(nc, ident_f32[:])
+        ident_bf16 = const.tile([P, P], BF16, name="ident_bf16")
+        make_identity(nc, ident_bf16[:])
+
+        def load_block(k):
+            rows = slice(k * TILES, (k + 1) * TILES)
+            x_sb = x_pool.tile([P, TILES * DI], BF16, name="x_sb")
+            nc.sync.dma_start(
+                out=x_sb[:].rearrange("p (t k) -> p t k", t=TILES), in_=x_rows[:, rows, :]
+            )
+            small_sb = small_pool.tile([P, N_SMALL * TILES * DH], BF16, name="small_sb")
+            small = small_sb[:].rearrange("p (a t d) -> p a t d", a=N_SMALL, t=TILES)
+            for a in range(N_SMALL):
+                nc.sync.dma_start(out=small[:, a], in_=small_rows[a][:, rows, :])
+            return x_sb, small
+
+        def transpose_words(words, copy_out, grouped_words):
+            turned = psum_in.tile([P, PASSES, HALVES, P], F32, name="turned", tag="in")
+            for g in range(PASSES):
+                for u in range(HALVES):
+                    first = (g * HALVES + u) * P
+                    nc.tensor.transpose(turned[:, g, u, :], words[:, first:first + P], ident_f32[:])
+            copy_out(out=grouped_words, in_=turned[:].rearrange("q g u r -> q g r u"))
+
+        loaded = {0: load_block(0)}
+
+        w_sb = const.tile([P, N_GATES * DI], BF16, name="w_sb")
+        w_chunks = w_sb[:].rearrange("p (c k) -> p c k", c=N_GATES)
+        for c in range(N_GATES):
+            nc.sync.dma_start(out=w_chunks[:, c, :], in_=weight_ih[c * P:(c + 1) * P, :])
+        loaded[1] = load_block(1)
+
+        small_w = const.tile([P, N_GATES, DH], BF16, name="small_w")
+        nc.scalar.dma_start(
+            out=small_w[:, 0:B0_G, :], in_=weight_hh.rearrange("(c p) d -> p c d", p=P)
+        )
+        for i, w in enumerate((weight_sh0, weight_sh1, weight_sh2)):
+            nc.scalar.dma_start(out=small_w[:, B0_G + i, :], in_=w)
+
+        bias_rows = const.tile([P, P], BF16, name="bias_rows")
+        nc.vector.memset(bias_rows[:], 0.0)
+        nc.scalar.dma_start(out=bias_rows[0:N_GATES, :], in_=bias_ih.rearrange("(r d) -> r d", d=DH))
+        nc.scalar.dma_start(
+            out=bias_rows[N_GATES:N_GATES + B0_G, :], in_=bias_hh.rearrange("(r d) -> r d", d=DH)
+        )
+        for i, b in enumerate((bias_sh0, bias_sh1, bias_sh2)):
+            row = N_GATES + B0_G + i
+            nc.scalar.dma_start(out=bias_rows[row:row + 1, :], in_=b.rearrange("(r d) -> r d", d=DH))
+
+        mask_bf16 = const.tile([P, ROWS_PER_PARTITION], BF16, name="mask_bf16")
+        nc.scalar.dma_start(out=mask_bf16[:], in_=mask.rearrange("(p j) -> p j", j=ROWS_PER_PARTITION))
+        m = const.tile([P, ROWS_PER_PARTITION], F32, name="m")
+        nc.vector.tensor_copy(out=m[:], in_=mask_bf16[:])
+
+        small_ps = psum_in.tile([P, N_GATES + 1, P], BF16, name="small_ps", tag="in")
+        for c in range(N_GATES):
+            nc.tensor.transpose(small_ps[:, c, :], small_w[:, c, :], ident_bf16[:])
+        nc.tensor.transpose(small_ps[:, N_GATES, :], bias_rows[:], ident_bf16[:])
+        small_wT = const.tile([P, N_GATES, DH], BF16, name="small_wT")
+        nc.vector.tensor_copy(out=small_wT[:], in_=small_ps[:, 0:N_GATES, :])
+        bias_cols = const.tile([P, 2 * N_GATES], F32, name="bias_cols")
+        nc.vector.tensor_copy(out=bias_cols[:], in_=small_ps[:, N_GATES, 0:2 * N_GATES])
+        bias = const.tile([P, N_GATES], F32, name="bias")
+        nc.vector.tensor_tensor(
+            out=bias[:], in0=bias_cols[:, 0:N_GATES], in1=bias_cols[:, N_GATES:2 * N_GATES], op=ALU.add
+        )
+
+        def transpose_and_quantise(k):
+            x_sb, small = loaded[k]
+            x_words = x_sb[:].bitcast(F32).rearrange("p (t w) -> p t w", t=TILES)
+            grouped = operand_pool.tile([P, PASSES * BLOCK * PACK], BF16, name="grouped", align_bytes=64)
+            grouped_words = grouped[:].bitcast(F32).rearrange(
+                "q (g r u) -> q g r u", g=PASSES, u=HALVES
+            )
+            for t in range(TILES):
+                transpose_words(x_words[:, t, :], nc.scalar.copy, grouped_words[:, :, t * P:(t + 1) * P, :])
+
+            turned_small = operand_pool.tile([P, (N_SMALL - 1) * BLOCK], BF16, name="turned_small")
+            turned_view = turned_small[:].rearrange("d (a t r) -> d a t r", a=N_SMALL - 1, t=TILES)
+            for pair in range(2):
+                pair_ps = psum_in.tile([P, 2, TILES, P], BF16, name="pair_ps", tag="in")
+                for i in range(2):
+                    for t in range(TILES):
+                        nc.tensor.transpose(pair_ps[:, i, t, :], small[:, 2 * pair + i, t, :], ident_bf16[:])
+                nc.scalar.copy(out=turned_view[:, 2 * pair:2 * pair + 2], in_=pair_ps[:])
+
+            x_codes = operand_pool.tile([P, PASSES * BLOCK], U32, name="x_codes", align_bytes=64)
+            x_scales = operand_pool.tile([P, PASSES * BLOCK], U8, name="x_scales", align_bytes=64)
+            nc.vector.quantize_mx(out=x_codes[:].bitcast(FP8X4), scales=x_scales[:], in_=grouped[:])
+            return x_codes, x_scales, turned_view
+
+        operands = {0: transpose_and_quantise(0)}
+
+        w_words = w_sb[:].bitcast(F32).rearrange("p (c w) -> p c w", c=N_GATES)
+        w_grouped = const.tile([P, N_GATES * PASSES * P * PACK], BF16, name="w_grouped", align_bytes=64)
+        w_grouped_words = w_grouped[:].bitcast(F32).rearrange(
+            "q (c g r u) -> q c g r u", c=N_GATES, g=PASSES, u=HALVES
+        )
+        for c in range(N_GATES):
+            copy_out = nc.scalar.copy if c % 2 == 0 else nc.vector.tensor_copy
+            transpose_words(w_words[:, c, :], copy_out, w_grouped_words[:, c])
+        w_codes = const.tile([P, N_GATES * CHUNK], U32, name="w_codes", align_bytes=64)
+        w_scales = const.tile([P, N_GATES * CHUNK], U8, name="w_scales", align_bytes=64)
+        for c in range(N_GATES):
+            nc.vector.quantize_mx(
+                out=w_codes[:, c * CHUNK:(c + 1) * CHUNK].bitcast(FP8X4),
+                scales=w_scales[:, c * CHUNK:(c + 1) * CHUNK],
+                in_=w_grouped[:, c * CHUNK * PACK:(c + 1) * CHUNK * PACK],
+            )
+
+        def gates(k):
+            x_codes, x_scales, turned_view = operands[k]
+            gate = gate_pool.tile([P, N_GATES, BLOCK], F32, name="gate")
+            for j in range(N_GATES):
+                source = turned_view[:, max(0, j - C_HAT)]
+                plain = psum_plain.tile([P, BLOCK], F32, name="plain")
+                nc.tensor.matmul(
+                    plain[:], lhsT=small_wT[:, j, :], rhs=source.rearrange("d t r -> d (t r)"),
+                    start=True, stop=True,
+                )
+                pre = pre_pool.tile([P, BLOCK], F32, name="pre")
+                nc.scalar.activation(out=pre[:], in_=plain[:], func=ACT.Identity, bias=bias[:, j:j + 1])
+
+                acc = psum_mx.tile([P, BLOCK], F32, name="acc")
+                for g in range(PASSES):
+                    w_cols = slice(j * CHUNK + g * P, j * CHUNK + (g + 1) * P)
+                    x_cols = slice(g * BLOCK, (g + 1) * BLOCK)
+                    nc.tensor.matmul_mx(
+                        out=acc[:],
+                        lhsT=w_codes[:, w_cols].bitcast(FP8X4),
+                        lhsT_scale=w_scales[:, w_cols],
+                        rhs=x_codes[:, x_cols].bitcast(FP8X4),
+                        rhs_scale=x_scales[:, x_cols],
+                        start=(g == 0),
+                        stop=(g == PASSES - 1),
+                    )
+                nc.vector.tensor_tensor(out=pre[:], in0=acc[:], in1=pre[:], op=ALU.add)
+                nc.scalar.activation(
+                    out=gate[:, j, :], in_=pre[:], func=ACT.Tanh if j == C_HAT else ACT.Sigmoid
+                )
+            i_tanh = gate_pool.tile([P, BLOCK], F32, name="i_tanh")
+            nc.vector.tensor_tensor(out=i_tanh[:], in0=gate[:, I_G, :], in1=gate[:, C_HAT, :], op=ALU.mult)
+            b_less_o = gate_pool.tile([P, 3, BLOCK], F32, name="b_less_o")
+            nc.vector.tensor_tensor(
+                out=b_less_o[:], in0=gate[:, B0_G:N_GATES, :],
+                in1=gate[:, O_G:O_G + 1, :].to_broadcast([P, 3, BLOCK]), op=ALU.subtract,
+            )
+            return gate, i_tanh, b_less_o
+
+        def to_rows(features):
+            rows_ps = psum_back.tile([P, TILES, DH], F32, name="rows_ps")
+            for t in range(TILES):
+                nc.tensor.transpose(rows_ps[:, t, :], features[:, t * P:(t + 1) * P], ident_f32[:])
+            return rows_ps
+
+        def finish(k):
+            gate, i_tanh, b_less_o = gated[k]
+            c_rows = loaded[k][1][:, C_SLOT]
+            h_out, c_out, s0_out, s1_out, s2_out = [
+                out_pool.tile([P, TILES, DH], F32, name=name)
+                for name in ("h_out", "c_out", "s0_out", "s1_out", "s2_out")
+            ]
+
+            f_rows = to_rows(gate[:, F_G, :])
+            i_tanh_rows = to_rows(i_tanh[:])
+            f_c = finish_pool.tile([P, TILES, DH], F32, name="f_c")
+            for t in range(TILES):
+                m_t = m[:, k * TILES + t:k * TILES + t + 1]
+                nc.vector.scalar_tensor_tensor(
+                    out=f_c[:, t, :], in0=f_rows[:, t, :], scalar=m_t, in1=c_rows[:, t, :],
+                    op0=ALU.mult, op1=ALU.mult,
+                )
+            for t in range(TILES):
+                m_t = m[:, k * TILES + t:k * TILES + t + 1]
+                nc.vector.scalar_tensor_tensor(
+                    out=c_out[:, t, :], in0=i_tanh_rows[:, t, :], scalar=m_t, in1=f_c[:, t, :],
+                    op0=ALU.mult, op1=ALU.add,
+                )
+            o_rows = to_rows(gate[:, O_G, :])
+            g0_rows = to_rows(b_less_o[:, 0, :])
+
+            tanh_c = finish_pool.tile([P, TILES, DH], F32, name="tanh_c")
+            nc.scalar.activation(out=tanh_c[:], in_=c_out[:], func=ACT.Tanh)
+            tc_rows = finish_pool.tile([P, TILES, DH], F32, name="tc_rows")
+            for t in range(TILES):
+                m_t = m[:, k * TILES + t:k * TILES + t + 1]
+                nc.scalar.activation(out=tc_rows[:, t, :], in_=tanh_c[:, t, :], func=ACT.Copy, scale=m_t)
+
+            nc.vector.tensor_tensor(out=h_out[:], in0=o_rows[:], in1=tc_rows[:], op=ALU.mult)
+            nc.vector.scalar_tensor_tensor(
+                out=s0_out[:], in0=g0_rows[:], scalar=1.0, in1=tc_rows[:], op0=ALU.add, op1=ALU.mult
+            )
+            g1_rows = to_rows(b_less_o[:, 1, :])
+            g2_rows = to_rows(b_less_o[:, 2, :])
+            s1_sum = finish_pool.tile([P, TILES, DH], F32, name="s1_sum")
+            nc.vector.scalar_tensor_tensor(
+                out=s1_sum[:], in0=g1_rows[:], scalar=2.0, in1=s0_out[:], op0=ALU.add, op1=ALU.subtract
+            )
+            s2_part = finish_pool.tile([P, TILES, DH], F32, name="s2_part")
+            nc.vector.scalar_tensor_tensor(
+                out=s2_part[:], in0=s0_out[:], scalar=-2.0, in1=g2_rows[:], op0=ALU.mult, op1=ALU.add
+            )
+            nc.vector.scalar_tensor_tensor(
+                out=s1_out[:], in0=s1_sum[:], scalar=0.5, in1=tc_rows[:], op0=ALU.mult, op1=ALU.mult
+            )
+            s2_sum = finish_pool.tile([P, TILES, DH], F32, name="s2_sum")
+            nc.vector.scalar_tensor_tensor(
+                out=s2_sum[:], in0=s2_part[:], scalar=3.0, in1=s1_out[:], op0=ALU.add, op1=ALU.subtract
+            )
+            nc.vector.scalar_tensor_tensor(
+                out=s2_out[:], in0=s2_sum[:], scalar=1.0 / 3.0, in1=tc_rows[:], op0=ALU.mult, op1=ALU.mult
+            )
+
+            rows = slice(k * TILES, (k + 1) * TILES)
+            for dst, result in zip(out_rows, (h_out, c_out, s0_out, s1_out, s2_out)):
+                nc.sync.dma_start(out=dst[:, rows, :], in_=result[:])
+
+        gated = {}
+        for k in range(N_BLOCKS):
+            if k + 2 < N_BLOCKS:
+                loaded[k + 2] = load_block(k + 2)
+            if k + 1 < N_BLOCKS:
+                operands[k + 1] = transpose_and_quantise(k + 1)
+            gated[k] = gates(k)
+            if k >= 1:
+                finish(k - 1)
+        finish(N_BLOCKS - 1)

@@ -25,12 +25,14 @@ ROWS_PER_PARTITION = B // P
 TILES = 4
 BLOCK = TILES * P
 N_BLOCKS = B // BLOCK
+N_STEPS = N_BLOCKS * N_GATES
 PACK = 4
 PASSES = DI // (P * PACK)
 HALVES = 2
 CHUNK = PASSES * P
 N_SMALL = 5
 C_SLOT = 4
+W_AHEAD = 2
 
 FLOPS = 2 * B * N_GATES * DH * (DI + DH)
 
@@ -48,12 +50,13 @@ def tile_share_lstm_cell_pa_t_kernel(
         a.rearrange("(p j) d -> p j d", j=ROWS_PER_PARTITION)
         for a in (h_minors, s0, s1, s2, c_minors)
     ]
-    out_rows = [
+    h_dram, c_dram, s0_dram, s1_dram, s2_dram = [
         a.rearrange("(p j) d -> p j d", j=ROWS_PER_PARTITION)
         for a in (out_0, out_1, out_2, out_3, out_4)
     ]
 
     with ExitStack() as stack:
+        stack.enter_context(tc.manual_schedule())
         const = stack.enter_context(tc.tile_pool(name="const", bufs=1))
         x_pool = stack.enter_context(tc.tile_pool(name="x_pool", bufs=3))
         small_pool = stack.enter_context(tc.tile_pool(name="small_pool", bufs=4))
@@ -67,38 +70,294 @@ def tile_share_lstm_cell_pa_t_kernel(
         psum_mx = stack.enter_context(tc.psum_pool(name="psum_mx", bufs=2))
         psum_back = stack.enter_context(tc.psum_pool(name="psum_back", bufs=2))
 
+        held = {}
+
+        def live(k):
+            return 0 <= k < N_BLOCKS
+
+        def block_rows(k):
+            return slice(k * TILES, (k + 1) * TILES)
+
+        def load_x(k):
+            if not live(k):
+                return
+            x_sb = x_pool.tile([P, TILES * DI], BF16, name="x_sb")
+            for t in range(TILES):
+                nc.sync.dma_start(out=x_sb[:, t * DI:(t + 1) * DI], in_=x_rows[:, k * TILES + t, :])
+            held["x_words", k] = x_sb[:].bitcast(F32).rearrange("p (t w) -> p t w", t=TILES)
+
+        def load_small(k):
+            if not live(k):
+                return
+            small_sb = small_pool.tile([P, N_SMALL * TILES * DH], BF16, name="small_sb")
+            small = small_sb[:].rearrange("p (a t d) -> p a t d", a=N_SMALL, t=TILES)
+            for a in range(N_SMALL):
+                nc.sync.dma_start(out=small[:, a], in_=small_rows[a][:, block_rows(k), :])
+            held["small", k] = small
+
+        w_sb = const.tile([P, N_GATES * DI], BF16, name="w_sb")
+        w_words = w_sb[:].bitcast(F32).rearrange("p (c w) -> p c w", c=N_GATES)
+
+        def load_weights(c):
+            nc.sync.dma_start(out=w_sb[:, c * DI:(c + 1) * DI], in_=weight_ih[c * P:(c + 1) * P, :])
+
+        def turn_words(words, pool, tag):
+            turned = pool.tile([P, PASSES, HALVES, P], F32, name="turned", tag=tag)
+            for g in range(PASSES):
+                for u in range(HALVES):
+                    first = (g * HALVES + u) * P
+                    nc.tensor.transpose(turned[:, g, u, :], words[:, first:first + P], ident_f32[:])
+            return turned[:].rearrange("q g u r -> q g r u")
+
+        def turn_x(k, t):
+            if live(k):
+                held["x_ps", k, t] = turn_words(held["x_words", k][:, t, :], psum_in, "in")
+
+        def copy_x(k, t, copy_out):
+            if not live(k):
+                return
+            if t == 0:
+                grouped = operand_pool.tile([P, PASSES * BLOCK * PACK], BF16, name="grouped", align_bytes=64)
+                held["grouped", k] = grouped
+            grouped_words = held["grouped", k][:].bitcast(F32).rearrange(
+                "q (g r u) -> q g r u", g=PASSES, u=HALVES
+            )
+            copy_out(out=grouped_words[:, :, t * P:(t + 1) * P, :], in_=held["x_ps", k, t])
+
+        def quantise_x(k):
+            if not live(k):
+                return
+            x_codes = operand_pool.tile([P, PASSES * BLOCK], U32, name="x_codes", align_bytes=64)
+            x_scales = operand_pool.tile([P, PASSES * BLOCK], U8, name="x_scales", align_bytes=64)
+            nc.vector.quantize_mx(
+                out=x_codes[:].bitcast(FP8X4), scales=x_scales[:], in_=held["grouped", k][:]
+            )
+            held["x_codes", k] = x_codes
+            held["x_scales", k] = x_scales
+
+        def turn_pair(k, pair):
+            if not live(k):
+                return
+            pair_ps = psum_in.tile([P, 2, TILES, P], BF16, name="pair_ps", tag="in")
+            for i in range(2):
+                for t in range(TILES):
+                    nc.tensor.transpose(
+                        pair_ps[:, i, t, :], held["small", k][:, 2 * pair + i, t, :], ident_bf16[:]
+                    )
+            held["pair_ps", k, pair] = pair_ps
+
+        def copy_pair(k, pair):
+            if not live(k):
+                return
+            if pair == 0:
+                turned_small = operand_pool.tile([P, (N_SMALL - 1) * BLOCK], BF16, name="turned_small")
+                held["turned_small", k] = turned_small[:].rearrange(
+                    "d (a r) -> d a r", a=N_SMALL - 1
+                )
+            nc.scalar.copy(
+                out=held["turned_small", k][:, 2 * pair:2 * pair + 2, :],
+                in_=held["pair_ps", k, pair][:].rearrange("d a t r -> d a (t r)"),
+            )
+
+        w_grouped = const.tile([P, N_GATES * CHUNK * PACK], BF16, name="w_grouped", align_bytes=64)
+        w_grouped_words = w_grouped[:].bitcast(F32).rearrange(
+            "q (c g r u) -> q c g r u", c=N_GATES, g=PASSES, u=HALVES
+        )
+        w_codes = const.tile([P, N_GATES * CHUNK], U32, name="w_codes", align_bytes=64)
+        w_scales = const.tile([P, N_GATES * CHUNK], U8, name="w_scales", align_bytes=64)
+
+        def prepare_weights(c):
+            copy_out = nc.scalar.copy if c % 2 == 0 else nc.vector.tensor_copy
+            copy_out(out=w_grouped_words[:, c], in_=turn_words(w_words[:, c, :], psum_back, "back"))
+            nc.vector.quantize_mx(
+                out=w_codes[:, c * CHUNK:(c + 1) * CHUNK].bitcast(FP8X4),
+                scales=w_scales[:, c * CHUNK:(c + 1) * CHUNK],
+                in_=w_grouped[:, c * CHUNK * PACK:(c + 1) * CHUNK * PACK],
+            )
+
+        def gate_matmuls(n):
+            if not 0 <= n < N_STEPS:
+                return
+            k, j = divmod(n, N_GATES)
+            plain = psum_plain.tile([P, BLOCK], F32, name="plain")
+            nc.tensor.matmul(
+                plain[:], lhsT=small_wT[:, j, :], rhs=held["turned_small", k][:, max(0, j - C_HAT), :],
+                start=True, stop=True,
+            )
+            acc = psum_mx.tile([P, BLOCK], F32, name="acc")
+            for g in range(PASSES):
+                w_cols = slice(j * CHUNK + g * P, j * CHUNK + (g + 1) * P)
+                x_cols = slice(g * BLOCK, (g + 1) * BLOCK)
+                nc.tensor.matmul_mx(
+                    out=acc[:],
+                    lhsT=w_codes[:, w_cols].bitcast(FP8X4),
+                    lhsT_scale=w_scales[:, w_cols],
+                    rhs=held["x_codes", k][:, x_cols].bitcast(FP8X4),
+                    rhs_scale=held["x_scales", k][:, x_cols],
+                    start=(g == 0),
+                    stop=(g == PASSES - 1),
+                )
+            held["plain", n] = plain
+            held["acc", n] = acc
+
+        def gate_sum(n):
+            if not 0 <= n < N_STEPS:
+                return
+            j = n % N_GATES
+            pre = pre_pool.tile([P, BLOCK], F32, name="pre")
+            nc.scalar.activation(out=pre[:], in_=held["plain", n][:], func=ACT.Identity, bias=bias[:, j:j + 1])
+            nc.vector.tensor_tensor(out=pre[:], in0=held["acc", n][:], in1=pre[:], op=ALU.add)
+            held["pre", n] = pre
+
+        def gate_function(n):
+            if not 0 <= n < N_STEPS:
+                return
+            k, j = divmod(n, N_GATES)
+            if j == 0:
+                held["gate", k] = gate_pool.tile([P, N_GATES, BLOCK], F32, name="gate")
+            if j == B0_G:
+                held["b_less_o", k] = gate_pool.tile([P, 3, BLOCK], F32, name="b_less_o")
+            gate = held["gate", k]
+            nc.scalar.activation(
+                out=gate[:, j, :], in_=held["pre", n][:], func=ACT.Tanh if j == C_HAT else ACT.Sigmoid
+            )
+            if j == C_HAT:
+                i_tanh = gate_pool.tile([P, BLOCK], F32, name="i_tanh")
+                nc.gpsimd.tensor_tensor(out=i_tanh[:], in0=gate[:, I_G, :], in1=gate[:, C_HAT, :], op=ALU.mult)
+                held["i_tanh", k] = i_tanh
+            if j >= B0_G:
+                nc.gpsimd.tensor_tensor(
+                    out=held["b_less_o", k][:, j - B0_G, :], in0=gate[:, j, :], in1=gate[:, O_G, :],
+                    op=ALU.subtract,
+                )
+
+        def gate_step(k, j):
+            n = k * N_GATES + j
+            if n + W_AHEAD < N_GATES:
+                prepare_weights(n + W_AHEAD)
+            gate_matmuls(n)
+            gate_sum(n - 1)
+            gate_function(n - 2)
+
+        def turn_back(k, name, features):
+            rows_ps = psum_back.tile([P, TILES, DH], F32, name="rows_ps", tag="back")
+            for t in range(TILES):
+                nc.tensor.transpose(rows_ps[:, t, :], features[:, t * P:(t + 1) * P], ident_f32[:])
+            held[name, k] = rows_ps
+
+        def turn_back_cell(k):
+            if live(k):
+                turn_back(k, "f_rows", held["gate", k][:, F_G, :])
+                turn_back(k, "i_tanh_rows", held["i_tanh", k][:])
+
+        def turn_back_first(k):
+            if live(k):
+                turn_back(k, "o_rows", held["gate", k][:, O_G, :])
+                turn_back(k, "g0_rows", held["b_less_o", k][:, 0, :])
+
+        def turn_back_last(k):
+            if live(k):
+                turn_back(k, "g1_rows", held["b_less_o", k][:, 1, :])
+                turn_back(k, "g2_rows", held["b_less_o", k][:, 2, :])
+
+        def new_rows(pool, name, k):
+            held[name, k] = pool.tile([P, TILES, DH], F32, name=name)
+            return held[name, k]
+
+        def mask_rows(k):
+            return m[:, block_rows(k)].unsqueeze(2).to_broadcast([P, TILES, DH])
+
+        def store(dram, k, name):
+            nc.sync.dma_start(out=dram[:, block_rows(k), :], in_=held[name, k][:])
+
+        def cell_product(k):
+            if live(k):
+                nc.vector.tensor_tensor(
+                    out=new_rows(finish_pool, "f_c", k)[:], in0=held["f_rows", k][:],
+                    in1=held["small", k][:, C_SLOT], op=ALU.mult,
+                )
+
+        def cell_state(k):
+            if live(k):
+                nc.vector.tensor_tensor(
+                    out=new_rows(finish_pool, "c_sum", k)[:], in0=held["i_tanh_rows", k][:],
+                    in1=held["f_c", k][:], op=ALU.add,
+                )
+                nc.gpsimd.tensor_tensor(
+                    out=new_rows(out_pool, "c_out", k)[:], in0=held["c_sum", k][:], in1=mask_rows(k), op=ALU.mult
+                )
+
+        def cell_tanh(k):
+            if live(k):
+                nc.scalar.activation(
+                    out=new_rows(finish_pool, "tanh_c", k)[:], in_=held["c_out", k][:], func=ACT.Tanh
+                )
+                nc.gpsimd.tensor_tensor(
+                    out=new_rows(finish_pool, "tc_rows", k)[:], in0=held["tanh_c", k][:], in1=mask_rows(k),
+                    op=ALU.mult,
+                )
+
+        def output_h(k):
+            if live(k):
+                nc.vector.tensor_tensor(
+                    out=new_rows(out_pool, "h_out", k)[:], in0=held["o_rows", k][:], in1=held["tc_rows", k][:],
+                    op=ALU.mult,
+                )
+
+        def output_s0(k):
+            if live(k):
+                nc.vector.scalar_tensor_tensor(
+                    out=new_rows(out_pool, "s0_out", k)[:], in0=held["g0_rows", k][:], scalar=1.0,
+                    in1=held["tc_rows", k][:], op0=ALU.add, op1=ALU.mult,
+                )
+                store(h_dram, k, "h_out")
+                store(c_dram, k, "c_out")
+                store(s0_dram, k, "s0_out")
+
+        def sums_s1_s2(k):
+            if live(k):
+                nc.vector.scalar_tensor_tensor(
+                    out=new_rows(finish_pool, "s1_sum", k)[:], in0=held["g1_rows", k][:], scalar=2.0,
+                    in1=held["s0_out", k][:], op0=ALU.add, op1=ALU.subtract,
+                )
+                nc.vector.scalar_tensor_tensor(
+                    out=new_rows(finish_pool, "s2_part", k)[:], in0=held["s0_out", k][:], scalar=-2.0,
+                    in1=held["g2_rows", k][:], op0=ALU.mult, op1=ALU.add,
+                )
+
+        def output_s1(k):
+            if live(k):
+                nc.vector.scalar_tensor_tensor(
+                    out=new_rows(out_pool, "s1_out", k)[:], in0=held["s1_sum", k][:], scalar=0.5,
+                    in1=held["tc_rows", k][:], op0=ALU.mult, op1=ALU.mult,
+                )
+                nc.vector.scalar_tensor_tensor(
+                    out=new_rows(finish_pool, "s2_sum", k)[:], in0=held["s2_part", k][:], scalar=3.0,
+                    in1=held["s1_out", k][:], op0=ALU.add, op1=ALU.subtract,
+                )
+
+        def output_s2(k):
+            if live(k):
+                nc.vector.scalar_tensor_tensor(
+                    out=new_rows(out_pool, "s2_out", k)[:], in0=held["s2_sum", k][:], scalar=1.0 / 3.0,
+                    in1=held["tc_rows", k][:], op0=ALU.mult, op1=ALU.mult,
+                )
+                store(s1_dram, k, "s1_out")
+                store(s2_dram, k, "s2_out")
+
         ident_f32 = const.tile([P, P], F32, name="ident_f32")
         make_identity(nc, ident_f32[:])
         ident_bf16 = const.tile([P, P], BF16, name="ident_bf16")
         make_identity(nc, ident_bf16[:])
 
-        def load_block(k):
-            rows = slice(k * TILES, (k + 1) * TILES)
-            x_sb = x_pool.tile([P, TILES * DI], BF16, name="x_sb")
-            nc.sync.dma_start(
-                out=x_sb[:].rearrange("p (t k) -> p t k", t=TILES), in_=x_rows[:, rows, :]
-            )
-            small_sb = small_pool.tile([P, N_SMALL * TILES * DH], BF16, name="small_sb")
-            small = small_sb[:].rearrange("p (a t d) -> p a t d", a=N_SMALL, t=TILES)
-            for a in range(N_SMALL):
-                nc.sync.dma_start(out=small[:, a], in_=small_rows[a][:, rows, :])
-            return x_sb, small
-
-        def transpose_words(words, copy_out, grouped_words):
-            turned = psum_in.tile([P, PASSES, HALVES, P], F32, name="turned", tag="in")
-            for g in range(PASSES):
-                for u in range(HALVES):
-                    first = (g * HALVES + u) * P
-                    nc.tensor.transpose(turned[:, g, u, :], words[:, first:first + P], ident_f32[:])
-            copy_out(out=grouped_words, in_=turned[:].rearrange("q g u r -> q g r u"))
-
-        loaded = {0: load_block(0)}
-
-        w_sb = const.tile([P, N_GATES * DI], BF16, name="w_sb")
-        w_chunks = w_sb[:].rearrange("p (c k) -> p c k", c=N_GATES)
-        for c in range(N_GATES):
-            nc.sync.dma_start(out=w_chunks[:, c, :], in_=weight_ih[c * P:(c + 1) * P, :])
-        loaded[1] = load_block(1)
+        load_x(0)
+        for c in range(W_AHEAD):
+            load_weights(c)
+        load_small(0)
+        for c in range(W_AHEAD, N_GATES):
+            load_weights(c)
+        load_x(1)
+        load_small(1)
 
         small_w = const.tile([P, N_GATES, DH], BF16, name="small_w")
         nc.scalar.dma_start(
@@ -106,7 +365,6 @@ def tile_share_lstm_cell_pa_t_kernel(
         )
         for i, w in enumerate((weight_sh0, weight_sh1, weight_sh2)):
             nc.scalar.dma_start(out=small_w[:, B0_G + i, :], in_=w)
-
         bias_rows = const.tile([P, P], BF16, name="bias_rows")
         nc.vector.memset(bias_rows[:], 0.0)
         nc.scalar.dma_start(out=bias_rows[0:N_GATES, :], in_=bias_ih.rearrange("(r d) -> r d", d=DH))
@@ -116,11 +374,12 @@ def tile_share_lstm_cell_pa_t_kernel(
         for i, b in enumerate((bias_sh0, bias_sh1, bias_sh2)):
             row = N_GATES + B0_G + i
             nc.scalar.dma_start(out=bias_rows[row:row + 1, :], in_=b.rearrange("(r d) -> r d", d=DH))
-
         mask_bf16 = const.tile([P, ROWS_PER_PARTITION], BF16, name="mask_bf16")
         nc.scalar.dma_start(out=mask_bf16[:], in_=mask.rearrange("(p j) -> p j", j=ROWS_PER_PARTITION))
-        m = const.tile([P, ROWS_PER_PARTITION], F32, name="m")
-        nc.vector.tensor_copy(out=m[:], in_=mask_bf16[:])
+
+        for t in range(TILES):
+            turn_x(0, t)
+            copy_x(0, t, nc.scalar.copy if t % 2 == 0 else nc.vector.tensor_copy)
 
         small_ps = psum_in.tile([P, N_GATES + 1, P], BF16, name="small_ps", tag="in")
         for c in range(N_GATES):
@@ -134,164 +393,47 @@ def tile_share_lstm_cell_pa_t_kernel(
         nc.vector.tensor_tensor(
             out=bias[:], in0=bias_cols[:, 0:N_GATES], in1=bias_cols[:, N_GATES:2 * N_GATES], op=ALU.add
         )
+        m = const.tile([P, ROWS_PER_PARTITION], F32, name="m")
+        nc.vector.tensor_copy(out=m[:], in_=mask_bf16[:])
 
-        def transpose_and_quantise(k):
-            x_sb, small = loaded[k]
-            x_words = x_sb[:].bitcast(F32).rearrange("p (t w) -> p t w", t=TILES)
-            grouped = operand_pool.tile([P, PASSES * BLOCK * PACK], BF16, name="grouped", align_bytes=64)
-            grouped_words = grouped[:].bitcast(F32).rearrange(
-                "q (g r u) -> q g r u", g=PASSES, u=HALVES
-            )
-            for t in range(TILES):
-                transpose_words(x_words[:, t, :], nc.scalar.copy, grouped_words[:, :, t * P:(t + 1) * P, :])
+        quantise_x(0)
+        for c in range(W_AHEAD):
+            prepare_weights(c)
 
-            turned_small = operand_pool.tile([P, (N_SMALL - 1) * BLOCK], BF16, name="turned_small")
-            turned_view = turned_small[:].rearrange("d (a t r) -> d a t r", a=N_SMALL - 1, t=TILES)
-            for pair in range(2):
-                pair_ps = psum_in.tile([P, 2, TILES, P], BF16, name="pair_ps", tag="in")
-                for i in range(2):
-                    for t in range(TILES):
-                        nc.tensor.transpose(pair_ps[:, i, t, :], small[:, 2 * pair + i, t, :], ident_bf16[:])
-                nc.scalar.copy(out=turned_view[:, 2 * pair:2 * pair + 2], in_=pair_ps[:])
+        for k in range(N_BLOCKS + 2):
+            load_x(k + 2)
+            load_small(k + 2)
 
-            x_codes = operand_pool.tile([P, PASSES * BLOCK], U32, name="x_codes", align_bytes=64)
-            x_scales = operand_pool.tile([P, PASSES * BLOCK], U8, name="x_scales", align_bytes=64)
-            nc.vector.quantize_mx(out=x_codes[:].bitcast(FP8X4), scales=x_scales[:], in_=grouped[:])
-            return x_codes, x_scales, turned_view
+            turn_pair(k, 0)
+            turn_pair(k, 1)
+            turn_back_cell(k - 1)
+            copy_pair(k, 0)
+            gate_step(k, 0)
+            copy_pair(k, 1)
+            cell_product(k - 1)
+            gate_step(k, 1)
+            cell_state(k - 1)
+            gate_step(k, 2)
 
-        operands = {0: transpose_and_quantise(0)}
+            turn_x(k + 1, 0)
+            turn_x(k + 1, 1)
+            turn_back_last(k - 2)
+            gate_step(k, 3)
+            copy_x(k + 1, 0, nc.scalar.copy)
+            sums_s1_s2(k - 2)
+            gate_step(k, 4)
+            copy_x(k + 1, 1, nc.scalar.copy)
+            cell_tanh(k - 1)
+            output_s1(k - 2)
 
-        w_words = w_sb[:].bitcast(F32).rearrange("p (c w) -> p c w", c=N_GATES)
-        w_grouped = const.tile([P, N_GATES * PASSES * P * PACK], BF16, name="w_grouped", align_bytes=64)
-        w_grouped_words = w_grouped[:].bitcast(F32).rearrange(
-            "q (c g r u) -> q c g r u", c=N_GATES, g=PASSES, u=HALVES
-        )
-        for c in range(N_GATES):
-            copy_out = nc.scalar.copy if c % 2 == 0 else nc.vector.tensor_copy
-            transpose_words(w_words[:, c, :], copy_out, w_grouped_words[:, c])
-        w_codes = const.tile([P, N_GATES * CHUNK], U32, name="w_codes", align_bytes=64)
-        w_scales = const.tile([P, N_GATES * CHUNK], U8, name="w_scales", align_bytes=64)
-        for c in range(N_GATES):
-            nc.vector.quantize_mx(
-                out=w_codes[:, c * CHUNK:(c + 1) * CHUNK].bitcast(FP8X4),
-                scales=w_scales[:, c * CHUNK:(c + 1) * CHUNK],
-                in_=w_grouped[:, c * CHUNK * PACK:(c + 1) * CHUNK * PACK],
-            )
-
-        def gates(k):
-            x_codes, x_scales, turned_view = operands[k]
-            gate = gate_pool.tile([P, N_GATES, BLOCK], F32, name="gate")
-            for j in range(N_GATES):
-                source = turned_view[:, max(0, j - C_HAT)]
-                plain = psum_plain.tile([P, BLOCK], F32, name="plain")
-                nc.tensor.matmul(
-                    plain[:], lhsT=small_wT[:, j, :], rhs=source.rearrange("d t r -> d (t r)"),
-                    start=True, stop=True,
-                )
-                pre = pre_pool.tile([P, BLOCK], F32, name="pre")
-                nc.scalar.activation(out=pre[:], in_=plain[:], func=ACT.Identity, bias=bias[:, j:j + 1])
-
-                acc = psum_mx.tile([P, BLOCK], F32, name="acc")
-                for g in range(PASSES):
-                    w_cols = slice(j * CHUNK + g * P, j * CHUNK + (g + 1) * P)
-                    x_cols = slice(g * BLOCK, (g + 1) * BLOCK)
-                    nc.tensor.matmul_mx(
-                        out=acc[:],
-                        lhsT=w_codes[:, w_cols].bitcast(FP8X4),
-                        lhsT_scale=w_scales[:, w_cols],
-                        rhs=x_codes[:, x_cols].bitcast(FP8X4),
-                        rhs_scale=x_scales[:, x_cols],
-                        start=(g == 0),
-                        stop=(g == PASSES - 1),
-                    )
-                nc.vector.tensor_tensor(out=pre[:], in0=acc[:], in1=pre[:], op=ALU.add)
-                nc.scalar.activation(
-                    out=gate[:, j, :], in_=pre[:], func=ACT.Tanh if j == C_HAT else ACT.Sigmoid
-                )
-            i_tanh = gate_pool.tile([P, BLOCK], F32, name="i_tanh")
-            nc.vector.tensor_tensor(out=i_tanh[:], in0=gate[:, I_G, :], in1=gate[:, C_HAT, :], op=ALU.mult)
-            b_less_o = gate_pool.tile([P, 3, BLOCK], F32, name="b_less_o")
-            nc.vector.tensor_tensor(
-                out=b_less_o[:], in0=gate[:, B0_G:N_GATES, :],
-                in1=gate[:, O_G:O_G + 1, :].to_broadcast([P, 3, BLOCK]), op=ALU.subtract,
-            )
-            return gate, i_tanh, b_less_o
-
-        def to_rows(features):
-            rows_ps = psum_back.tile([P, TILES, DH], F32, name="rows_ps")
-            for t in range(TILES):
-                nc.tensor.transpose(rows_ps[:, t, :], features[:, t * P:(t + 1) * P], ident_f32[:])
-            return rows_ps
-
-        def finish(k):
-            gate, i_tanh, b_less_o = gated[k]
-            c_rows = loaded[k][1][:, C_SLOT]
-            h_out, c_out, s0_out, s1_out, s2_out = [
-                out_pool.tile([P, TILES, DH], F32, name=name)
-                for name in ("h_out", "c_out", "s0_out", "s1_out", "s2_out")
-            ]
-
-            f_rows = to_rows(gate[:, F_G, :])
-            i_tanh_rows = to_rows(i_tanh[:])
-            f_c = finish_pool.tile([P, TILES, DH], F32, name="f_c")
-            for t in range(TILES):
-                m_t = m[:, k * TILES + t:k * TILES + t + 1]
-                nc.vector.scalar_tensor_tensor(
-                    out=f_c[:, t, :], in0=f_rows[:, t, :], scalar=m_t, in1=c_rows[:, t, :],
-                    op0=ALU.mult, op1=ALU.mult,
-                )
-            for t in range(TILES):
-                m_t = m[:, k * TILES + t:k * TILES + t + 1]
-                nc.vector.scalar_tensor_tensor(
-                    out=c_out[:, t, :], in0=i_tanh_rows[:, t, :], scalar=m_t, in1=f_c[:, t, :],
-                    op0=ALU.mult, op1=ALU.add,
-                )
-            o_rows = to_rows(gate[:, O_G, :])
-            g0_rows = to_rows(b_less_o[:, 0, :])
-
-            tanh_c = finish_pool.tile([P, TILES, DH], F32, name="tanh_c")
-            nc.scalar.activation(out=tanh_c[:], in_=c_out[:], func=ACT.Tanh)
-            tc_rows = finish_pool.tile([P, TILES, DH], F32, name="tc_rows")
-            for t in range(TILES):
-                m_t = m[:, k * TILES + t:k * TILES + t + 1]
-                nc.scalar.activation(out=tc_rows[:, t, :], in_=tanh_c[:, t, :], func=ACT.Copy, scale=m_t)
-
-            nc.vector.tensor_tensor(out=h_out[:], in0=o_rows[:], in1=tc_rows[:], op=ALU.mult)
-            nc.vector.scalar_tensor_tensor(
-                out=s0_out[:], in0=g0_rows[:], scalar=1.0, in1=tc_rows[:], op0=ALU.add, op1=ALU.mult
-            )
-            g1_rows = to_rows(b_less_o[:, 1, :])
-            g2_rows = to_rows(b_less_o[:, 2, :])
-            s1_sum = finish_pool.tile([P, TILES, DH], F32, name="s1_sum")
-            nc.vector.scalar_tensor_tensor(
-                out=s1_sum[:], in0=g1_rows[:], scalar=2.0, in1=s0_out[:], op0=ALU.add, op1=ALU.subtract
-            )
-            s2_part = finish_pool.tile([P, TILES, DH], F32, name="s2_part")
-            nc.vector.scalar_tensor_tensor(
-                out=s2_part[:], in0=s0_out[:], scalar=-2.0, in1=g2_rows[:], op0=ALU.mult, op1=ALU.add
-            )
-            nc.vector.scalar_tensor_tensor(
-                out=s1_out[:], in0=s1_sum[:], scalar=0.5, in1=tc_rows[:], op0=ALU.mult, op1=ALU.mult
-            )
-            s2_sum = finish_pool.tile([P, TILES, DH], F32, name="s2_sum")
-            nc.vector.scalar_tensor_tensor(
-                out=s2_sum[:], in0=s2_part[:], scalar=3.0, in1=s1_out[:], op0=ALU.add, op1=ALU.subtract
-            )
-            nc.vector.scalar_tensor_tensor(
-                out=s2_out[:], in0=s2_sum[:], scalar=1.0 / 3.0, in1=tc_rows[:], op0=ALU.mult, op1=ALU.mult
-            )
-
-            rows = slice(k * TILES, (k + 1) * TILES)
-            for dst, result in zip(out_rows, (h_out, c_out, s0_out, s1_out, s2_out)):
-                nc.sync.dma_start(out=dst[:, rows, :], in_=result[:])
-
-        gated = {}
-        for k in range(N_BLOCKS):
-            if k + 2 < N_BLOCKS:
-                loaded[k + 2] = load_block(k + 2)
-            if k + 1 < N_BLOCKS:
-                operands[k + 1] = transpose_and_quantise(k + 1)
-            gated[k] = gates(k)
-            if k >= 1:
-                finish(k - 1)
-        finish(N_BLOCKS - 1)
+            turn_x(k + 1, 2)
+            turn_x(k + 1, 3)
+            turn_back_first(k - 1)
+            gate_step(k, 5)
+            copy_x(k + 1, 2, nc.scalar.copy)
+            copy_x(k + 1, 3, nc.vector.tensor_copy)
+            output_h(k - 1)
+            output_s2(k - 2)
+            gate_step(k, 6)
+            output_s0(k - 1)
+            quantise_x(k + 1)

@@ -78,11 +78,13 @@ def tile_share_lstm_cell_pa_t_kernel(
         def block_rows(k):
             return slice(k * TILES, (k + 1) * TILES)
 
-        def load_x(k):
+        def load_x(k, tiles):
             if not live(k):
                 return
-            x_sb = x_pool.tile([P, TILES * DI], BF16, name="x_sb")
-            for t in range(TILES):
+            if tiles[0] == 0:
+                held["x_sb", k] = x_pool.tile([P, TILES * DI], BF16, name="x_sb")
+            x_sb = held["x_sb", k]
+            for t in tiles:
                 nc.sync.dma_start(out=x_sb[:, t * DI:(t + 1) * DI], in_=x_rows[:, k * TILES + t, :])
             held["x_words", k] = x_sb[:].bitcast(F32).rearrange("p (t w) -> p t w", t=TILES)
 
@@ -203,9 +205,8 @@ def tile_share_lstm_cell_pa_t_kernel(
         def gate_sum(n):
             if not 0 <= n < N_STEPS:
                 return
-            j = n % N_GATES
             pre = pre_pool.tile([P, BLOCK], F32, name="pre")
-            nc.scalar.activation(out=pre[:], in_=held["plain", n][:], func=ACT.Identity, bias=bias[:, j:j + 1])
+            nc.scalar.copy(out=pre[:], in_=held["plain", n][:])
             nc.vector.tensor_tensor(out=pre[:], in0=held["acc", n][:], in1=pre[:], op=ALU.add)
             held["pre", n] = pre
 
@@ -219,7 +220,8 @@ def tile_share_lstm_cell_pa_t_kernel(
                 held["b_less_o", k] = gate_pool.tile([P, 3, BLOCK], F32, name="b_less_o")
             gate = held["gate", k]
             nc.scalar.activation(
-                out=gate[:, j, :], in_=held["pre", n][:], func=ACT.Tanh if j == C_HAT else ACT.Sigmoid
+                out=gate[:, j, :], in_=held["pre", n][:], func=ACT.Tanh if j == C_HAT else ACT.Sigmoid,
+                bias=bias[:, j:j + 1],
             )
             if j == C_HAT:
                 i_tanh = gate_pool.tile([P, BLOCK], F32, name="i_tanh")
@@ -264,38 +266,39 @@ def tile_share_lstm_cell_pa_t_kernel(
             held[name, k] = pool.tile([P, TILES, DH], F32, name=name)
             return held[name, k]
 
-        def mask_rows(k):
-            return m[:, block_rows(k)].unsqueeze(2).to_broadcast([P, TILES, DH])
+        def mask_of(k, t):
+            return m[:, k * TILES + t:k * TILES + t + 1]
 
         def store(dram, k, name):
             nc.sync.dma_start(out=dram[:, block_rows(k), :], in_=held[name, k][:])
 
         def cell_product(k):
             if live(k):
-                nc.vector.tensor_tensor(
-                    out=new_rows(finish_pool, "f_c", k)[:], in0=held["f_rows", k][:],
-                    in1=held["small", k][:, C_SLOT], op=ALU.mult,
-                )
+                f_c = new_rows(finish_pool, "f_c", k)
+                for t in range(TILES):
+                    nc.vector.scalar_tensor_tensor(
+                        out=f_c[:, t, :], in0=held["f_rows", k][:, t, :], scalar=mask_of(k, t),
+                        in1=held["small", k][:, C_SLOT, t, :], op0=ALU.mult, op1=ALU.mult,
+                    )
 
         def cell_state(k):
             if live(k):
-                nc.vector.tensor_tensor(
-                    out=new_rows(finish_pool, "c_sum", k)[:], in0=held["i_tanh_rows", k][:],
-                    in1=held["f_c", k][:], op=ALU.add,
-                )
-                nc.gpsimd.tensor_tensor(
-                    out=new_rows(out_pool, "c_out", k)[:], in0=held["c_sum", k][:], in1=mask_rows(k), op=ALU.mult
-                )
+                c_out = new_rows(out_pool, "c_out", k)
+                for t in range(TILES):
+                    nc.vector.scalar_tensor_tensor(
+                        out=c_out[:, t, :], in0=held["i_tanh_rows", k][:, t, :], scalar=mask_of(k, t),
+                        in1=held["f_c", k][:, t, :], op0=ALU.mult, op1=ALU.add,
+                    )
 
         def cell_tanh(k):
             if live(k):
-                nc.scalar.activation(
-                    out=new_rows(finish_pool, "tanh_c", k)[:], in_=held["c_out", k][:], func=ACT.Tanh
-                )
-                nc.gpsimd.tensor_tensor(
-                    out=new_rows(finish_pool, "tc_rows", k)[:], in0=held["tanh_c", k][:], in1=mask_rows(k),
-                    op=ALU.mult,
-                )
+                tanh_c = new_rows(finish_pool, "tanh_c", k)
+                nc.scalar.activation(out=tanh_c[:], in_=held["c_out", k][:], func=ACT.Tanh)
+                tc_rows = new_rows(finish_pool, "tc_rows", k)
+                for t in range(TILES):
+                    nc.scalar.activation(
+                        out=tc_rows[:, t, :], in_=tanh_c[:, t, :], func=ACT.Copy, scale=mask_of(k, t)
+                    )
 
         def output_h(k):
             if live(k):
@@ -350,13 +353,17 @@ def tile_share_lstm_cell_pa_t_kernel(
         ident_bf16 = const.tile([P, P], BF16, name="ident_bf16")
         make_identity(nc, ident_bf16[:])
 
-        load_x(0)
-        for c in range(W_AHEAD):
-            load_weights(c)
+        load_x(0, (0, 1, 2, 3))
+        load_weights(0)
+        load_weights(1)
         load_small(0)
-        for c in range(W_AHEAD, N_GATES):
-            load_weights(c)
-        load_x(1)
+        load_x(1, (0, 1))
+        load_weights(2)
+        load_weights(3)
+        load_x(1, (2, 3))
+        load_weights(4)
+        load_weights(5)
+        load_weights(6)
         load_small(1)
 
         small_w = const.tile([P, N_GATES, DH], BF16, name="small_w")
@@ -399,41 +406,44 @@ def tile_share_lstm_cell_pa_t_kernel(
         quantise_x(0)
         for c in range(W_AHEAD):
             prepare_weights(c)
+        for pair in range(2):
+            turn_pair(0, pair)
+            copy_pair(0, pair)
 
         for k in range(N_BLOCKS + 2):
-            load_x(k + 2)
+            load_x(k + 2, (0, 1, 2, 3))
             load_small(k + 2)
-
-            turn_pair(k, 0)
-            turn_pair(k, 1)
-            turn_back_cell(k - 1)
-            copy_pair(k, 0)
-            gate_step(k, 0)
-            copy_pair(k, 1)
-            cell_product(k - 1)
-            gate_step(k, 1)
-            cell_state(k - 1)
-            gate_step(k, 2)
 
             turn_x(k + 1, 0)
             turn_x(k + 1, 1)
-            turn_back_last(k - 2)
-            gate_step(k, 3)
+            turn_back_cell(k - 1)
+            gate_step(k, 0)
             copy_x(k + 1, 0, nc.scalar.copy)
-            sums_s1_s2(k - 2)
-            gate_step(k, 4)
-            copy_x(k + 1, 1, nc.scalar.copy)
-            cell_tanh(k - 1)
-            output_s1(k - 2)
+            cell_product(k - 1)
+            copy_x(k + 1, 1, nc.vector.tensor_copy)
+            gate_step(k, 1)
+            cell_state(k - 1)
 
             turn_x(k + 1, 2)
             turn_x(k + 1, 3)
+            turn_back_last(k - 2)
+            gate_step(k, 2)
+            copy_x(k + 1, 2, nc.scalar.copy)
+            sums_s1_s2(k - 2)
+            copy_x(k + 1, 3, nc.vector.tensor_copy)
+            gate_step(k, 3)
+            output_s1(k - 2)
+            gate_step(k, 4)
+            cell_tanh(k - 1)
+            output_s2(k - 2)
+            quantise_x(k + 1)
+
+            turn_pair(k + 1, 0)
+            turn_pair(k + 1, 1)
             turn_back_first(k - 1)
             gate_step(k, 5)
-            copy_x(k + 1, 2, nc.scalar.copy)
-            copy_x(k + 1, 3, nc.vector.tensor_copy)
+            copy_pair(k + 1, 0)
             output_h(k - 1)
-            output_s2(k - 2)
             gate_step(k, 6)
+            copy_pair(k + 1, 1)
             output_s0(k - 1)
-            quantise_x(k + 1)

@@ -78,15 +78,17 @@ def tile_share_lstm_cell_pa_t_kernel(
         def block_rows(k):
             return slice(k * TILES, (k + 1) * TILES)
 
-        def load_x(k, tiles):
+        def load_x(k, first, count):
             if not live(k):
                 return
-            if tiles[0] == 0:
-                held["x_sb", k] = x_pool.tile([P, TILES * DI], BF16, name="x_sb")
-            x_sb = held["x_sb", k]
-            for t in tiles:
-                nc.sync.dma_start(out=x_sb[:, t * DI:(t + 1) * DI], in_=x_rows[:, k * TILES + t, :])
-            held["x_words", k] = x_sb[:].bitcast(F32).rearrange("p (t w) -> p t w", t=TILES)
+            if first == 0:
+                x_sb = x_pool.tile([P, TILES * DI], BF16, name="x_sb")
+                held["x_tiles", k] = x_sb[:].rearrange("p (t k) -> p t k", t=TILES)
+                held["x_words", k] = x_sb[:].bitcast(F32).rearrange("p (t w) -> p t w", t=TILES)
+            nc.sync.dma_start(
+                out=held["x_tiles", k][:, first:first + count, :],
+                in_=x_rows[:, k * TILES + first:k * TILES + first + count, :],
+            )
 
         def load_small(k):
             if not live(k):
@@ -353,56 +355,47 @@ def tile_share_lstm_cell_pa_t_kernel(
         ident_bf16 = const.tile([P, P], BF16, name="ident_bf16")
         make_identity(nc, ident_bf16[:])
 
-        load_x(0, (0, 1, 2, 3))
-        load_weights(0)
-        load_weights(1)
-        load_small(0)
-        load_x(1, (0, 1))
-        load_weights(2)
-        load_weights(3)
-        load_x(1, (2, 3))
-        load_weights(4)
-        load_weights(5)
-        load_weights(6)
-        load_small(1)
-
         small_w = const.tile([P, N_GATES, DH], BF16, name="small_w")
         nc.scalar.dma_start(
             out=small_w[:, 0:B0_G, :], in_=weight_hh.rearrange("(c p) d -> p c d", p=P)
         )
         for i, w in enumerate((weight_sh0, weight_sh1, weight_sh2)):
             nc.scalar.dma_start(out=small_w[:, B0_G + i, :], in_=w)
+
+        for t in range(TILES):
+            load_x(0, t, 1)
+        load_weights(0)
+        load_weights(1)
+        load_small(0)
         bias_rows = const.tile([P, P], BF16, name="bias_rows")
         nc.vector.memset(bias_rows[:], 0.0)
-        nc.scalar.dma_start(out=bias_rows[0:N_GATES, :], in_=bias_ih.rearrange("(r d) -> r d", d=DH))
-        nc.scalar.dma_start(
+        nc.sync.dma_start(out=bias_rows[0:N_GATES, :], in_=bias_ih.rearrange("(r d) -> r d", d=DH))
+        nc.sync.dma_start(
             out=bias_rows[N_GATES:N_GATES + B0_G, :], in_=bias_hh.rearrange("(r d) -> r d", d=DH)
         )
         for i, b in enumerate((bias_sh0, bias_sh1, bias_sh2)):
             row = N_GATES + B0_G + i
-            nc.scalar.dma_start(out=bias_rows[row:row + 1, :], in_=b.rearrange("(r d) -> r d", d=DH))
+            nc.sync.dma_start(out=bias_rows[row:row + 1, :], in_=b.rearrange("(r d) -> r d", d=DH))
+        load_x(1, 0, 2)
+        load_weights(2)
+        load_weights(3)
+        load_x(1, 2, 2)
+        load_weights(4)
+        load_weights(5)
+        load_weights(6)
+        load_small(1)
         mask_bf16 = const.tile([P, ROWS_PER_PARTITION], BF16, name="mask_bf16")
-        nc.scalar.dma_start(out=mask_bf16[:], in_=mask.rearrange("(p j) -> p j", j=ROWS_PER_PARTITION))
+        nc.sync.dma_start(out=mask_bf16[:], in_=mask.rearrange("(p j) -> p j", j=ROWS_PER_PARTITION))
+
+        small_ps = psum_in.tile([P, N_GATES, P], BF16, name="small_ps", tag="in")
+        for c in range(N_GATES):
+            nc.tensor.transpose(small_ps[:, c, :], small_w[:, c, :], ident_bf16[:])
+        small_wT = const.tile([P, N_GATES, DH], BF16, name="small_wT")
+        nc.vector.tensor_copy(out=small_wT[:], in_=small_ps[:])
 
         for t in range(TILES):
             turn_x(0, t)
             copy_x(0, t, nc.scalar.copy if t % 2 == 0 else nc.vector.tensor_copy)
-
-        small_ps = psum_in.tile([P, N_GATES + 1, P], BF16, name="small_ps", tag="in")
-        for c in range(N_GATES):
-            nc.tensor.transpose(small_ps[:, c, :], small_w[:, c, :], ident_bf16[:])
-        nc.tensor.transpose(small_ps[:, N_GATES, :], bias_rows[:], ident_bf16[:])
-        small_wT = const.tile([P, N_GATES, DH], BF16, name="small_wT")
-        nc.vector.tensor_copy(out=small_wT[:], in_=small_ps[:, 0:N_GATES, :])
-        bias_cols = const.tile([P, 2 * N_GATES], F32, name="bias_cols")
-        nc.vector.tensor_copy(out=bias_cols[:], in_=small_ps[:, N_GATES, 0:2 * N_GATES])
-        bias = const.tile([P, N_GATES], F32, name="bias")
-        nc.vector.tensor_tensor(
-            out=bias[:], in0=bias_cols[:, 0:N_GATES], in1=bias_cols[:, N_GATES:2 * N_GATES], op=ALU.add
-        )
-        m = const.tile([P, ROWS_PER_PARTITION], F32, name="m")
-        nc.vector.tensor_copy(out=m[:], in_=mask_bf16[:])
-
         quantise_x(0)
         for c in range(W_AHEAD):
             prepare_weights(c)
@@ -410,8 +403,19 @@ def tile_share_lstm_cell_pa_t_kernel(
             turn_pair(0, pair)
             copy_pair(0, pair)
 
+        bias_ps = psum_in.tile([P, P], BF16, name="bias_ps", tag="in")
+        nc.tensor.transpose(bias_ps[:], bias_rows[:], ident_bf16[:])
+        bias_cols = const.tile([P, 2 * N_GATES], F32, name="bias_cols")
+        nc.vector.tensor_copy(out=bias_cols[:], in_=bias_ps[:, 0:2 * N_GATES])
+        bias = const.tile([P, N_GATES], F32, name="bias")
+        nc.vector.tensor_tensor(
+            out=bias[:], in0=bias_cols[:, 0:N_GATES], in1=bias_cols[:, N_GATES:2 * N_GATES], op=ALU.add
+        )
+        m = const.tile([P, ROWS_PER_PARTITION], F32, name="m")
+        nc.gpsimd.tensor_copy(out=m[:], in_=mask_bf16[:])
+
         for k in range(N_BLOCKS + 2):
-            load_x(k + 2, (0, 1, 2, 3))
+            load_x(k + 2, 0, TILES)
             load_small(k + 2)
 
             turn_x(k + 1, 0)

from contextlib import ExitStack

import concourse.mybir as mybir
from concourse.masks import make_identity

F32 = mybir.dt.float32
BF16 = mybir.dt.bfloat16
U32 = mybir.dt.uint32
U8 = mybir.dt.uint8
FP8X4 = mybir.dt.float8_e4m3fn_x4
ACT = mybir.ActivationFunctionType
ALU = mybir.AluOpType

P = 128
B = 4096
DI = 1024
DH = 128
N_GATES = 7
I_G = 0
F_G = 1
O_G = 2
C_HAT = 3
B0_G = 4
ROWS_PER_PARTITION = B // P
TILES = 4
BLOCK = TILES * P
N_BLOCKS = B // BLOCK
N_STEPS = N_BLOCKS * N_GATES
PACK = 4
PASSES = DI // (P * PACK)
HALVES = 2
CHUNK = PASSES * P
N_SMALL = 5
C_SLOT = 4
W_AHEAD = 2

FLOPS = 2 * B * N_GATES * DH * (DI + DH)


def tile_share_lstm_cell_pa_t_kernel(
    tc, x, h_minors, c_minors, s0, s1, s2, mask,
    weight_ih, bias_ih, weight_hh, bias_hh,
    weight_sh0, bias_sh0, weight_sh1, bias_sh1, weight_sh2, bias_sh2,
    out_0, out_1, out_2, out_3, out_4,
):
    nc = tc.nc

    x_rows = x.rearrange("(p j) k -> p j k", j=ROWS_PER_PARTITION)
    small_rows = [
        a.rearrange("(p j) d -> p j d", j=ROWS_PER_PARTITION)
        for a in (h_minors, s0, s1, s2, c_minors)
    ]
    h_dram, c_dram, s0_dram, s1_dram, s2_dram = [
        a.rearrange("(p j) d -> p j d", j=ROWS_PER_PARTITION)
        for a in (out_0, out_1, out_2, out_3, out_4)
    ]

    with ExitStack() as stack:
        stack.enter_context(tc.manual_schedule())
        const = stack.enter_context(tc.tile_pool(name="const", bufs=1))
        x_pool = stack.enter_context(tc.tile_pool(name="x_pool", bufs=3))
        small_pool = stack.enter_context(tc.tile_pool(name="small_pool", bufs=4))
        operand_pool = stack.enter_context(tc.tile_pool(name="operand_pool", bufs=2))
        pre_pool = stack.enter_context(tc.tile_pool(name="pre_pool", bufs=4))
        gate_pool = stack.enter_context(tc.tile_pool(name="gate_pool", bufs=2))
        finish_pool = stack.enter_context(tc.tile_pool(name="finish_pool", bufs=2))
        out_pool = stack.enter_context(tc.tile_pool(name="out_pool", bufs=2))
        psum_in = stack.enter_context(tc.psum_pool(name="psum_in", bufs=2))
        psum_plain = stack.enter_context(tc.psum_pool(name="psum_plain", bufs=2))
        psum_mx = stack.enter_context(tc.psum_pool(name="psum_mx", bufs=2))
        psum_back = stack.enter_context(tc.psum_pool(name="psum_back", bufs=2))

        held = {}

        def live(k):
            return 0 <= k < N_BLOCKS

        def block_rows(k):
            return slice(k * TILES, (k + 1) * TILES)

        def load_x(k, first, count):
            if not live(k):
                return
            if first == 0:
                x_sb = x_pool.tile([P, TILES * DI], BF16, name="x_sb")
                held["x_tiles", k] = x_sb[:].rearrange("p (t k) -> p t k", t=TILES)
                held["x_words", k] = x_sb[:].bitcast(F32).rearrange("p (t w) -> p t w", t=TILES)
            nc.sync.dma_start(
                out=held["x_tiles", k][:, first:first + count, :],
                in_=x_rows[:, k * TILES + first:k * TILES + first + count, :],
            )

        def load_small(k):
            if not live(k):
                return
            small_sb = small_pool.tile([P, N_SMALL * TILES * DH], BF16, name="small_sb")
            small = small_sb[:].rearrange("p (a t d) -> p a t d", a=N_SMALL, t=TILES)
            for a in range(N_SMALL):
                nc.sync.dma_start(out=small[:, a], in_=small_rows[a][:, block_rows(k), :])
            held["small", k] = small

        w_sb = const.tile([P, N_GATES * DI], BF16, name="w_sb")
        w_words = w_sb[:].bitcast(F32).rearrange("p (c w) -> p c w", c=N_GATES)

        def load_weights(c):
            nc.sync.dma_start(out=w_sb[:, c * DI:(c + 1) * DI], in_=weight_ih[c * P:(c + 1) * P, :])

        def turn_words(words, pool, tag):
            turned = pool.tile([P, PASSES, HALVES, P], F32, name="turned", tag=tag)
            for g in range(PASSES):
                for u in range(HALVES):
                    first = (g * HALVES + u) * P
                    nc.tensor.transpose(turned[:, g, u, :], words[:, first:first + P], ident_f32[:])
            return turned[:].rearrange("q g u r -> q g r u")

        def turn_x(k, t):
            if live(k):
                held["x_ps", k, t] = turn_words(held["x_words", k][:, t, :], psum_in, "in")

        def copy_x(k, t, copy_out):
            if not live(k):
                return
            if t == 0:
                grouped = operand_pool.tile([P, PASSES * BLOCK * PACK], BF16, name="grouped", align_bytes=64)
                held["grouped", k] = grouped
            grouped_words = held["grouped", k][:].bitcast(F32).rearrange(
                "q (g r u) -> q g r u", g=PASSES, u=HALVES
            )
            copy_out(out=grouped_words[:, :, t * P:(t + 1) * P, :], in_=held["x_ps", k, t])

        def quantise_x(k):
            if not live(k):
                return
            x_codes = operand_pool.tile([P, PASSES * BLOCK], U32, name="x_codes", align_bytes=64)
            x_scales = operand_pool.tile([P, PASSES * BLOCK], U8, name="x_scales", align_bytes=64)
            nc.vector.quantize_mx(
                out=x_codes[:].bitcast(FP8X4), scales=x_scales[:], in_=held["grouped", k][:]
            )
            held["x_codes", k] = x_codes
            held["x_scales", k] = x_scales

        def turn_pair(k, pair):
            if not live(k):
                return
            pair_ps = psum_in.tile([P, 2, TILES, P], BF16, name="pair_ps", tag="in")
            for i in range(2):
                for t in range(TILES):
                    nc.tensor.transpose(
                        pair_ps[:, i, t, :], held["small", k][:, 2 * pair + i, t, :], ident_bf16[:]
                    )
            held["pair_ps", k, pair] = pair_ps

        def copy_pair(k, pair):
            if not live(k):
                return
            if pair == 0:
                turned_small = operand_pool.tile([P, (N_SMALL - 1) * BLOCK], BF16, name="turned_small")
                held["turned_small", k] = turned_small[:].rearrange(
                    "d (a r) -> d a r", a=N_SMALL - 1
                )
            nc.scalar.copy(
                out=held["turned_small", k][:, 2 * pair:2 * pair + 2, :],
                in_=held["pair_ps", k, pair][:].rearrange("d a t r -> d a (t r)"),
            )

        w_grouped = const.tile([P, N_GATES * CHUNK * PACK], BF16, name="w_grouped", align_bytes=64)
        w_grouped_words = w_grouped[:].bitcast(F32).rearrange(
            "q (c g r u) -> q c g r u", c=N_GATES, g=PASSES, u=HALVES
        )
        w_codes = const.tile([P, N_GATES * CHUNK], U32, name="w_codes", align_bytes=64)
        w_scales = const.tile([P, N_GATES * CHUNK], U8, name="w_scales", align_bytes=64)

        def prepare_weights(c):
            copy_out = nc.scalar.copy if c % 2 == 0 else nc.vector.tensor_copy
            copy_out(out=w_grouped_words[:, c], in_=turn_words(w_words[:, c, :], psum_back, "back"))
            nc.vector.quantize_mx(
                out=w_codes[:, c * CHUNK:(c + 1) * CHUNK].bitcast(FP8X4),
                scales=w_scales[:, c * CHUNK:(c + 1) * CHUNK],
                in_=w_grouped[:, c * CHUNK * PACK:(c + 1) * CHUNK * PACK],
            )

        def gate_matmuls(n):
            if not 0 <= n < N_STEPS:
                return
            k, j = divmod(n, N_GATES)
            plain = psum_plain.tile([P, BLOCK], F32, name="plain")
            nc.tensor.matmul(
                plain[:], lhsT=small_wT[:, j, :], rhs=held["turned_small", k][:, max(0, j - C_HAT), :],
                start=True, stop=True,
            )
            acc = psum_mx.tile([P, BLOCK], F32, name="acc")
            for g in range(PASSES):
                w_cols = slice(j * CHUNK + g * P, j * CHUNK + (g + 1) * P)
                x_cols = slice(g * BLOCK, (g + 1) * BLOCK)
                nc.tensor.matmul_mx(
                    out=acc[:],
                    lhsT=w_codes[:, w_cols].bitcast(FP8X4),
                    lhsT_scale=w_scales[:, w_cols],
                    rhs=held["x_codes", k][:, x_cols].bitcast(FP8X4),
                    rhs_scale=held["x_scales", k][:, x_cols],
                    start=(g == 0),
                    stop=(g == PASSES - 1),
                )
            held["plain", n] = plain
            held["acc", n] = acc

        def gate_sum(n):
            if not 0 <= n < N_STEPS:
                return
            pre = pre_pool.tile([P, BLOCK], F32, name="pre")
            nc.scalar.copy(out=pre[:], in_=held["plain", n][:])
            nc.vector.tensor_tensor(out=pre[:], in0=held["acc", n][:], in1=pre[:], op=ALU.add)
            held["pre", n] = pre

        def gate_function(n):
            if not 0 <= n < N_STEPS:
                return
            k, j = divmod(n, N_GATES)
            if j == 0:
                held["gate", k] = gate_pool.tile([P, N_GATES, BLOCK], F32, name="gate")
            if j == B0_G:
                held["b_less_o", k] = gate_pool.tile([P, 3, BLOCK], F32, name="b_less_o")
            gate = held["gate", k]
            nc.scalar.activation(
                out=gate[:, j, :], in_=held["pre", n][:], func=ACT.Tanh if j == C_HAT else ACT.Sigmoid,
                bias=bias[:, j:j + 1],
            )
            if j == C_HAT:
                i_tanh = gate_pool.tile([P, BLOCK], F32, name="i_tanh")
                nc.gpsimd.tensor_tensor(out=i_tanh[:], in0=gate[:, I_G, :], in1=gate[:, C_HAT, :], op=ALU.mult)
                held["i_tanh", k] = i_tanh
            if j >= B0_G:
                nc.gpsimd.tensor_tensor(
                    out=held["b_less_o", k][:, j - B0_G, :], in0=gate[:, j, :], in1=gate[:, O_G, :],
                    op=ALU.subtract,
                )

        def gate_step(k, j):
            n = k * N_GATES + j
            if n + W_AHEAD < N_GATES:
                prepare_weights(n + W_AHEAD)
            gate_matmuls(n)
            gate_sum(n - 1)
            gate_function(n - 2)

        def turn_back(k, name, features):
            rows_ps = psum_back.tile([P, TILES, DH], F32, name="rows_ps", tag="back")
            for t in range(TILES):
                nc.tensor.transpose(rows_ps[:, t, :], features[:, t * P:(t + 1) * P], ident_f32[:])
            held[name, k] = rows_ps

        def turn_back_cell(k):
            if live(k):
                turn_back(k, "f_rows", held["gate", k][:, F_G, :])
                turn_back(k, "i_tanh_rows", held["i_tanh", k][:])

        def turn_back_first(k):
            if live(k):
                turn_back(k, "o_rows", held["gate", k][:, O_G, :])
                turn_back(k, "g0_rows", held["b_less_o", k][:, 0, :])

        def turn_back_last(k):
            if live(k):
                turn_back(k, "g1_rows", held["b_less_o", k][:, 1, :])
                turn_back(k, "g2_rows", held["b_less_o", k][:, 2, :])

        def new_rows(pool, name, k):
            held[name, k] = pool.tile([P, TILES, DH], F32, name=name)
            return held[name, k]

        def mask_of(k, t):
            return m[:, k * TILES + t:k * TILES + t + 1]

        def store(dram, k, name):
            nc.sync.dma_start(out=dram[:, block_rows(k), :], in_=held[name, k][:])

        def cell_product(k):
            if live(k):
                f_c = new_rows(finish_pool, "f_c", k)
                for t in range(TILES):
                    nc.vector.scalar_tensor_tensor(
                        out=f_c[:, t, :], in0=held["f_rows", k][:, t, :], scalar=mask_of(k, t),
                        in1=held["small", k][:, C_SLOT, t, :], op0=ALU.mult, op1=ALU.mult,
                    )

        def cell_state(k):
            if live(k):
                c_out = new_rows(out_pool, "c_out", k)
                for t in range(TILES):
                    nc.vector.scalar_tensor_tensor(
                        out=c_out[:, t, :], in0=held["i_tanh_rows", k][:, t, :], scalar=mask_of(k, t),
                        in1=held["f_c", k][:, t, :], op0=ALU.mult, op1=ALU.add,
                    )

        def cell_tanh(k):
            if live(k):
                tanh_c = new_rows(finish_pool, "tanh_c", k)
                nc.scalar.activation(out=tanh_c[:], in_=held["c_out", k][:], func=ACT.Tanh)
                tc_rows = new_rows(finish_pool, "tc_rows", k)
                for t in range(TILES):
                    nc.scalar.activation(
                        out=tc_rows[:, t, :], in_=tanh_c[:, t, :], func=ACT.Copy, scale=mask_of(k, t)
                    )

        def output_h(k):
            if live(k):
                nc.vector.tensor_tensor(
                    out=new_rows(out_pool, "h_out", k)[:], in0=held["o_rows", k][:], in1=held["tc_rows", k][:],
                    op=ALU.mult,
                )

        def output_s0(k):
            if live(k):
                nc.vector.scalar_tensor_tensor(
                    out=new_rows(out_pool, "s0_out", k)[:], in0=held["g0_rows", k][:], scalar=1.0,
                    in1=held["tc_rows", k][:], op0=ALU.add, op1=ALU.mult,
                )
                store(h_dram, k, "h_out")
                store(c_dram, k, "c_out")
                store(s0_dram, k, "s0_out")

        def sums_s1_s2(k):
            if live(k):
                nc.vector.scalar_tensor_tensor(
                    out=new_rows(finish_pool, "s1_sum", k)[:], in0=held["g1_rows", k][:], scalar=2.0,
                    in1=held["s0_out", k][:], op0=ALU.add, op1=ALU.subtract,
                )
                nc.vector.scalar_tensor_tensor(
                    out=new_rows(finish_pool, "s2_part", k)[:], in0=held["s0_out", k][:], scalar=-2.0,
                    in1=held["g2_rows", k][:], op0=ALU.mult, op1=ALU.add,
                )

        def output_s1(k):
            if live(k):
                nc.vector.scalar_tensor_tensor(
                    out=new_rows(out_pool, "s1_out", k)[:], in0=held["s1_sum", k][:], scalar=0.5,
                    in1=held["tc_rows", k][:], op0=ALU.mult, op1=ALU.mult,
                )
                nc.vector.scalar_tensor_tensor(
                    out=new_rows(finish_pool, "s2_sum", k)[:], in0=held["s2_part", k][:], scalar=3.0,
                    in1=held["s1_out", k][:], op0=ALU.add, op1=ALU.subtract,
                )

        def output_s2(k):
            if live(k):
                nc.vector.scalar_tensor_tensor(
                    out=new_rows(out_pool, "s2_out", k)[:], in0=held["s2_sum", k][:], scalar=1.0 / 3.0,
                    in1=held["tc_rows", k][:], op0=ALU.mult, op1=ALU.mult,
                )
                store(s1_dram, k, "s1_out")
                store(s2_dram, k, "s2_out")

        ident_f32 = const.tile([P, P], F32, name="ident_f32")
        make_identity(nc, ident_f32[:])
        ident_bf16 = const.tile([P, P], BF16, name="ident_bf16")
        make_identity(nc, ident_bf16[:])

        small_w = const.tile([P, N_GATES, DH], BF16, name="small_w")
        nc.scalar.dma_start(
            out=small_w[:, 0:B0_G, :], in_=weight_hh.rearrange("(c p) d -> p c d", p=P)
        )
        for i, w in enumerate((weight_sh0, weight_sh1, weight_sh2)):
            nc.scalar.dma_start(out=small_w[:, B0_G + i, :], in_=w)

        for t in range(TILES):
            load_x(0, t, 1)
        load_weights(0)
        load_weights(1)
        load_small(0)
        bias_rows = const.tile([P, P], BF16, name="bias_rows")
        nc.vector.memset(bias_rows[:], 0.0)
        nc.sync.dma_start(out=bias_rows[0:N_GATES, :], in_=bias_ih.rearrange("(r d) -> r d", d=DH))
        nc.sync.dma_start(
            out=bias_rows[N_GATES:N_GATES + B0_G, :], in_=bias_hh.rearrange("(r d) -> r d", d=DH)
        )
        for i, b in enumerate((bias_sh0, bias_sh1, bias_sh2)):
            row = N_GATES + B0_G + i
            nc.sync.dma_start(out=bias_rows[row:row + 1, :], in_=b.rearrange("(r d) -> r d", d=DH))
        load_x(1, 0, 2)
        load_weights(2)
        load_weights(3)
        load_x(1, 2, 2)
        load_weights(4)
        load_weights(5)
        load_weights(6)
        load_small(1)
        mask_bf16 = const.tile([P, ROWS_PER_PARTITION], BF16, name="mask_bf16")
        nc.sync.dma_start(out=mask_bf16[:], in_=mask.rearrange("(p j) -> p j", j=ROWS_PER_PARTITION))

        small_ps = psum_in.tile([P, N_GATES, P], BF16, name="small_ps", tag="in")
        for c in range(N_GATES):
            nc.tensor.transpose(small_ps[:, c, :], small_w[:, c, :], ident_bf16[:])
        small_wT = const.tile([P, N_GATES, DH], BF16, name="small_wT")
        nc.vector.tensor_copy(out=small_wT[:], in_=small_ps[:])

        for t in range(TILES):
            turn_x(0, t)
            copy_x(0, t, nc.scalar.copy if t % 2 == 0 else nc.vector.tensor_copy)
        quantise_x(0)
        for c in range(W_AHEAD):
            prepare_weights(c)
        for pair in range(2):
            turn_pair(0, pair)
            copy_pair(0, pair)

        bias_ps = psum_in.tile([P, P], BF16, name="bias_ps", tag="in")
        nc.tensor.transpose(bias_ps[:], bias_rows[:], ident_bf16[:])
        bias_cols = const.tile([P, 2 * N_GATES], F32, name="bias_cols")
        nc.vector.tensor_copy(out=bias_cols[:], in_=bias_ps[:, 0:2 * N_GATES])
        bias = const.tile([P, N_GATES], F32, name="bias")
        nc.vector.tensor_tensor(
            out=bias[:], in0=bias_cols[:, 0:N_GATES], in1=bias_cols[:, N_GATES:2 * N_GATES], op=ALU.add
        )
        m = const.tile([P, ROWS_PER_PARTITION], F32, name="m")
        nc.gpsimd.tensor_copy(out=m[:], in_=mask_bf16[:])

        for k in range(N_BLOCKS + 2):
            load_x(k + 2, 0, TILES)
            load_small(k + 2)

            turn_x(k + 1, 0)
            turn_x(k + 1, 1)
            turn_back_cell(k - 1)
            gate_step(k, 0)
            copy_x(k + 1, 0, nc.scalar.copy)
            cell_product(k - 1)
            copy_x(k + 1, 1, nc.vector.tensor_copy)
            gate_step(k, 1)
            cell_state(k - 1)

            turn_x(k + 1, 2)
            turn_x(k + 1, 3)
            turn_back_last(k - 2)
            gate_step(k, 2)
            copy_x(k + 1, 2, nc.scalar.copy)
            sums_s1_s2(k - 2)
            copy_x(k + 1, 3, nc.vector.tensor_copy)
            gate_step(k, 3)
            output_s1(k - 2)
            gate_step(k, 4)
            cell_tanh(k - 1)
            output_s2(k - 2)
            quantise_x(k + 1)

            turn_pair(k + 1, 0)
            turn_pair(k + 1, 1)
            turn_back_first(k - 1)
            gate_step(k, 5)
            copy_pair(k + 1, 0)
            output_h(k - 1)
            gate_step(k, 6)
            copy_pair(k + 1, 1)
            output_s0(k - 1)
